import numpy as np
import ml_dtypes


def mxq(x, axis, fmt="e4m3"):
    dtype, down = {"e4m3": (ml_dtypes.float8_e4m3fn, 7), "e5m2": (ml_dtypes.float8_e5m2, 14)}[fmt]
    v = np.moveaxis(np.asarray(x, np.float32).astype(ml_dtypes.bfloat16).astype(np.float64), axis, -1)
    blocks = v.reshape(v.shape[:-1] + (-1, 32))
    amax = np.abs(blocks).max(-1, keepdims=True)
    byte = np.maximum(np.where(amax > 0, np.frexp(amax)[1] - 1 + 127, 0) - down, 1)
    scale = np.exp2(byte - 127.0)
    codes = (blocks / scale).astype(np.float32).astype(dtype).astype(np.float64)
    return np.moveaxis((codes * scale).reshape(v.shape), -1, axis)


WIDE = False


def mx_kscale(k):
    if not WIDE:
        return np.ones(k)
    levels = np.array([10, -10, 5, -5, 0])
    a = np.random.permutation(np.resize(levels, k // 512 * 4)).reshape(k // 512, 4)
    idx = np.arange(k)
    return np.exp2(a[idx // 512, idx % 128 // 32])


BF16 = ml_dtypes.bfloat16


def bf(x):
    return np.asarray(x, np.float32).astype(BF16)


def f64(x):
    return np.asarray(x).astype(np.float64)


B, M, K, N = 2, 512, 2048, 2048
THRESHOLD = 1e-6
TILE = 64
LIVE = 4e-6
QUIET = 8e-7


def mask_inactive_tiles(a, threshold, tile=TILE):
    nb, m, k = a.shape
    blocks = np.abs(a).reshape(nb, m // tile, tile, k // tile, tile)
    active = blocks.max(axis=(2, 4)) > threshold
    mask = np.repeat(np.repeat(active, tile, axis=1), tile, axis=2)
    return a * mask.astype(a.dtype)


def setup_inputs():
    s = mx_kscale(K)
    lv = LIVE / s.min()
    live = np.random.random((B, M // TILE, K // TILE)) < 0.75
    livem = np.repeat(np.repeat(live, TILE, axis=1), TILE, axis=2)
    a_live = np.random.standard_normal((B, M, K)) * lv * s
    a_quiet = np.random.uniform(-QUIET, QUIET, (B, M, K))
    return {"a": bf(np.where(livem, a_live, a_quiet)),
            "b": bf(np.random.standard_normal((B, K, N)) / np.sqrt(K) / lv / s[:, None])}


def reference(a, b):
    a_sp = mask_inactive_tiles(f64(a), THRESHOLD)
    return mxq(a_sp, 2, "e4m3") @ mxq(f64(b), 1, "e4m3")

@@ -1,0 +1,190 @@
+from contextlib import ExitStack
+
+import concourse.mybir as mybir
+from concourse.masks import make_identity
+
+F32 = mybir.dt.float32
+BF16 = mybir.dt.bfloat16
+I32 = mybir.dt.int32
+U32 = mybir.dt.uint32
+U8 = mybir.dt.uint8
+FP8X4 = mybir.dt.float8_e4m3fn_x4
+ALU = mybir.AluOpType
+
+B, M, K, N = 2, 512, 2048, 2048
+THRESHOLD = 1e-6
+P = 128
+PACK = 4
+K_PASS = P * PACK
+PASSES = K // K_PASS
+M_TILES = M // P
+N_HALF = 1024
+N_TILE = 512
+FLOPS = 2 * B * M * K * N
+
+S_COLS_FIRST = 1024
+S_COLS = 384
+FIRST_CHUNKS = 3
+
+
+def tile_sparsebmm_kernel(tc, a, b, out):
+    nc = tc.nc
+    with ExitStack() as ctx:
+        const = ctx.enter_context(tc.tile_pool(name="const", bufs=1))
+        araw_pool = ctx.enter_context(tc.tile_pool(name="araw", bufs=8))
+        awork = ctx.enter_context(tc.tile_pool(name="awork", bufs=3))
+        braw_pool = ctx.enter_context(tc.tile_pool(name="braw", bufs=8))
+        bgrp_pool = ctx.enter_context(tc.tile_pool(name="bgrp", bufs=3))
+        bq_pool = ctx.enter_context(tc.tile_pool(name="bq", bufs=6))
+        stage_pool = ctx.enter_context(tc.tile_pool(name="stage", bufs=6))
+        psum = ctx.enter_context(tc.psum_pool(name="psum", bufs=8))
+
+        ident = const.tile([P, P], F32, name="ident")
+        make_identity(nc, ident[:])
+        sel = const.tile([P, 32], BF16, name="sel")
+        nc.gpsimd.memset(sel[:], 0.0)
+        nc.gpsimd.memset(sel[0:64, 0:1], 1.0)
+        nc.gpsimd.memset(sel[64:128, 1:2], 1.0)
+        spread = const.tile([P, 4, P], BF16, name="spread")
+        nc.gpsimd.memset(spread[:], 0.0)
+        for q in range(4):
+            nc.gpsimd.memset(spread[0:64, q, 32 * q : 32 * q + 16], 1.0)
+            nc.gpsimd.memset(spread[64:128, q, 32 * q + 16 : 32 * q + 32], 1.0)
+
+        a_codes = const.tile([P, B * M_TILES, K_PASS], U32, name="a_codes", align_bytes=64)
+        a_scales = const.tile([P, B * M_TILES, K_PASS], U8, name="a_scales", align_bytes=64)
+
+        a_raws = []
+        for g in range(B * M_TILES):
+            bi, mt = divmod(g, M_TILES)
+            a_raw = araw_pool.tile([P, K], BF16, name="a_raw", tag="a_raw")
+            nc.sync.dma_start(out=a_raw[:], in_=a[bi, mt * P : (mt + 1) * P, :])
+            a_raws.append(a_raw)
+
+        for g in range(B * M_TILES):
+            a_raw = a_raws[g]
+            big = awork.tile([P, K], BF16, name="big", tag="big")
+            nc.vector.tensor_scalar(
+                out=big[:].bitcast(I32),
+                in0=a_raw[:].bitcast(I32),
+                scalar1=0x7FFF7FFF,
+                scalar2=None,
+                op0=ALU.bitwise_and,
+            )
+            nc.vector.tensor_scalar(
+                out=big[:], in0=big[:], scalar1=THRESHOLD, scalar2=None, op0=ALU.is_gt
+            )
+            cnt = psum.tile([P, 16, 32], F32, name="cnt", tag="bank")
+            for kc in range(16):
+                nc.tensor.matmul(
+                    out=cnt[:, kc, :],
+                    lhsT=big[:, kc * P : (kc + 1) * P],
+                    rhs=sel[:],
+                    start=True,
+                    stop=True,
+                )
+            cnt_sb = awork.tile([P, 16, 8], BF16, name="cnt_sb", tag="cnt_sb")
+            nc.vector.tensor_copy(out=cnt_sb[:], in_=cnt[:, :, 0:8])
+            tot = psum.tile([P, PASSES, 8], F32, name="tot", tag="bank")
+            cnt_by_q = cnt_sb[:].rearrange("p (c q) e -> p q c e", q=4)
+            for q in range(4):
+                nc.tensor.matmul(
+                    out=tot[:],
+                    lhsT=spread[:, q, :],
+                    rhs=cnt_by_q[:, q],
+                    start=(q == 0),
+                    stop=(q == 3),
+                )
+            keep = awork.tile([P, PASSES, 2], BF16, name="keep", tag="keep")
+            nc.vector.tensor_scalar(
+                out=keep[:], in0=tot[:, :, 0:2], scalar1=0.5, scalar2=None, op0=ALU.is_gt
+            )
+
+            words = a_raw[:].bitcast(F32).rearrange("p (c w u) -> p c u w", c=PASSES, u=2)
+            grouped = awork.tile([P, PACK * K_PASS], BF16, name="a_grouped", tag="a_grouped", align_bytes=64)
+            grouped_w = grouped[:].bitcast(F32).rearrange("p (c m u) -> p c m u", c=PASSES, u=2)
+            for h in range(2):
+                xt = psum.tile([P, 2, 2, P], F32, name="xt", tag="bank")
+                for ci in range(2):
+                    for u in range(2):
+                        nc.tensor.transpose(xt[:, ci, u, :], words[:, 2 * h + ci, u, :], ident[:])
+                nc.scalar.copy(
+                    out=grouped_w[:, 2 * h : 2 * h + 2],
+                    in_=xt[:].rearrange("p c u m -> p c m u"),
+                )
+            by_tile = grouped[:].rearrange("p (t e) -> p t e", e=256)
+            nc.vector.tensor_tensor(
+                out=by_tile,
+                in0=by_tile,
+                in1=keep[:].rearrange("p c j -> p (c j)").unsqueeze(2).to_broadcast([P, 8, 256]),
+                op=ALU.mult,
+            )
+            nc.vector.quantize_mx(
+                out=a_codes[:, g, :].bitcast(FP8X4),
+                scales=a_scales[:, g, :],
+                in_=grouped[:],
+            )
+
+        chunk = 0
+        for bi in range(B):
+            for nh in range(N // N_HALF):
+                last_round = bi == B - 1 and nh == N // N_HALF - 1
+                cols = slice(nh * N_HALF, (nh + 1) * N_HALF)
+                accs = []
+                for i in range(M_TILES * 2):
+                    acc = psum.tile([P, N_TILE], F32, name="acc", tag="bank")
+                    accs.append(acc)
+                for c in range(PASSES):
+                    b_raw = braw_pool.tile([P, PACK, N_HALF], BF16, name="b_raw", tag="b_raw")
+                    nc.sync.dma_start(
+                        out=b_raw[:],
+                        in_=b[bi, c * K_PASS : (c + 1) * K_PASS, cols].rearrange(
+                            "(p t) n -> p t n", t=PACK
+                        ),
+                    )
+                    b_grp = bgrp_pool.tile([P, N_HALF, PACK], BF16, name="b_grp", tag="b_grp", align_bytes=64)
+                    s_cols = S_COLS_FIRST if chunk < FIRST_CHUNKS else S_COLS
+                    v_cols = N_HALF - s_cols
+                    if v_cols > 0:
+                        nc.vector.tensor_copy(
+                            out=b_grp[:, 0:v_cols, :].rearrange("p (c i) t -> p c t i", i=4),
+                            in_=b_raw[:, :, 0:v_cols].rearrange("p t (c i) -> p c t i", i=4),
+                        )
+                    nc.scalar.copy(
+                        out=b_grp[:, v_cols:N_HALF, :].rearrange("p (c i) t -> p c t i", i=4),
+                        in_=b_raw[:, :, v_cols:N_HALF].rearrange("p t (c i) -> p c t i", i=4),
+                    )
+                    b_codes = bq_pool.tile([P, N_HALF], U32, name="b_codes", tag="b_codes", align_bytes=64)
+                    b_scales = bq_pool.tile([P, N_HALF], U8, name="b_scales", tag="b_scales", align_bytes=64)
+                    nc.vector.quantize_mx(
+                        out=b_codes[:].bitcast(FP8X4),
+                        scales=b_scales[:],
+                        in_=b_grp[:].rearrange("p n t -> p (n t)"),
+                    )
+                    for mt in range(M_TILES):
+                        g = bi * M_TILES + mt
+                        for nt in range(2):
+                            nc.tensor.matmul_mx(
+                                out=accs[2 * mt + nt][:],
+                                lhsT=a_codes[:, g, c * P : (c + 1) * P].bitcast(FP8X4),
+                                lhsT_scale=a_scales[:, g, c * P : (c + 1) * P],
+                                rhs=b_codes[:, nt * N_TILE : (nt + 1) * N_TILE].bitcast(FP8X4),
+                                rhs_scale=b_scales[:, nt * N_TILE : (nt + 1) * N_TILE],
+                                start=(c == 0),
+                                stop=(c == PASSES - 1),
+                            )
+                    chunk += 1
+                for mt in range(M_TILES):
+                    stage = stage_pool.tile([P, N_HALF], F32, name="stage", tag="stage")
+                    on_vector = last_round and mt % 2 == 1
+                    for nt in range(2):
+                        dst = stage[:, nt * N_TILE : (nt + 1) * N_TILE]
+                        if on_vector:
+                            nc.vector.tensor_copy(out=dst, in_=accs[2 * mt + nt][:])
+                        else:
+                            nc.scalar.copy(out=dst, in_=accs[2 * mt + nt][:])
+                    rows = out[bi, mt * P : (mt + 1) * P, cols]
+                    if on_vector:
+                        nc.sync.dma_start(out=rows, in_=stage[:])
+                    else:
+                        nc.scalar.dma_start(out=rows, in_=stage[:])

@@ -18,26 +18,35 @@ PACK = 4
 K_PASS = P * PACK
 PASSES = K // K_PASS
 M_TILES = M // P
-N_HALF = 1024
 N_TILE = 512
 FLOPS = 2 * B * M * K * N
 
-S_COLS_FIRST = 1024
-S_COLS = 384
-FIRST_CHUNKS = 3
+ROUNDS = ((0, 0, 1024), (0, 1024, 1024), (1, 0, 1024), (1, 1024, 512), (1, 1536, 512))
+S_COLS = (640, 1024, 640, 640, 384, 320, 320, 576, 384, 320, 320, 576, 288, 288, 0, 0, 160, 160, 96, 96)
+S_PIECE = 512
+B_RAW_BUFS = 8
+S_AHEAD = 3
+V_AHEAD = 2
+Q_AHEAD = 1
+PIN = True
 
 
 def tile_sparsebmm_kernel(tc, a, b, out):
     nc = tc.nc
+    n_chunks = len(ROUNDS) * PASSES
     with ExitStack() as ctx:
         const = ctx.enter_context(tc.tile_pool(name="const", bufs=1))
-        araw_pool = ctx.enter_context(tc.tile_pool(name="araw", bufs=8))
-        awork = ctx.enter_context(tc.tile_pool(name="awork", bufs=3))
-        braw_pool = ctx.enter_context(tc.tile_pool(name="braw", bufs=8))
-        bgrp_pool = ctx.enter_context(tc.tile_pool(name="bgrp", bufs=3))
+        araw_pool = ctx.enter_context(tc.tile_pool(name="araw", bufs=4))
+        awork = ctx.enter_context(tc.tile_pool(name="awork", bufs=2))
+        agrp_pool = ctx.enter_context(tc.tile_pool(name="agrp", bufs=6))
+        keep_pool = ctx.enter_context(tc.tile_pool(name="keep", bufs=8))
+        braw_pool = ctx.enter_context(tc.tile_pool(name="braw", bufs=B_RAW_BUFS))
+        bgrp_pool = ctx.enter_context(tc.tile_pool(name="bgrp", bufs=5))
         bq_pool = ctx.enter_context(tc.tile_pool(name="bq", bufs=6))
-        stage_pool = ctx.enter_context(tc.tile_pool(name="stage", bufs=6))
+        stage_pool = ctx.enter_context(tc.tile_pool(name="stage", bufs=4))
         psum = ctx.enter_context(tc.psum_pool(name="psum", bufs=8))
+        if PIN:
+            ctx.enter_context(tc.manual_schedule())
 
         ident = const.tile([P, P], F32, name="ident")
         make_identity(nc, ident[:])
@@ -54,55 +63,19 @@ def tile_sparsebmm_kernel(tc, a, b, out):
         a_codes = const.tile([P, B * M_TILES, K_PASS], U32, name="a_codes", align_bytes=64)
         a_scales = const.tile([P, B * M_TILES, K_PASS], U8, name="a_scales", align_bytes=64)
 
-        a_raws = []
-        for g in range(B * M_TILES):
+        a_raw, big, a_grp, cnt, tot, keep = {}, {}, {}, {}, {}, {}
+        b_raw, b_grp, b_q = {}, {}, {}
+        done = {"rs": 0, "rv": 0, "q": 0}
+
+        def load_a(g):
             bi, mt = divmod(g, M_TILES)
-            a_raw = araw_pool.tile([P, K], BF16, name="a_raw", tag="a_raw")
-            nc.sync.dma_start(out=a_raw[:], in_=a[bi, mt * P : (mt + 1) * P, :])
-            a_raws.append(a_raw)
+            a_raw[g] = araw_pool.tile([P, K], BF16, name="a_raw", tag="a_raw")
+            nc.sync.dma_start(out=a_raw[g][:], in_=a[bi, mt * P : (mt + 1) * P, :])
 
-        for g in range(B * M_TILES):
-            a_raw = a_raws[g]
-            big = awork.tile([P, K], BF16, name="big", tag="big")
-            nc.vector.tensor_scalar(
-                out=big[:].bitcast(I32),
-                in0=a_raw[:].bitcast(I32),
-                scalar1=0x7FFF7FFF,
-                scalar2=None,
-                op0=ALU.bitwise_and,
-            )
-            nc.vector.tensor_scalar(
-                out=big[:], in0=big[:], scalar1=THRESHOLD, scalar2=None, op0=ALU.is_gt
-            )
-            cnt = psum.tile([P, 16, 32], F32, name="cnt", tag="bank")
-            for kc in range(16):
-                nc.tensor.matmul(
-                    out=cnt[:, kc, :],
-                    lhsT=big[:, kc * P : (kc + 1) * P],
-                    rhs=sel[:],
-                    start=True,
-                    stop=True,
-                )
-            cnt_sb = awork.tile([P, 16, 8], BF16, name="cnt_sb", tag="cnt_sb")
-            nc.vector.tensor_copy(out=cnt_sb[:], in_=cnt[:, :, 0:8])
-            tot = psum.tile([P, PASSES, 8], F32, name="tot", tag="bank")
-            cnt_by_q = cnt_sb[:].rearrange("p (c q) e -> p q c e", q=4)
-            for q in range(4):
-                nc.tensor.matmul(
-                    out=tot[:],
-                    lhsT=spread[:, q, :],
-                    rhs=cnt_by_q[:, q],
-                    start=(q == 0),
-                    stop=(q == 3),
-                )
-            keep = awork.tile([P, PASSES, 2], BF16, name="keep", tag="keep")
-            nc.vector.tensor_scalar(
-                out=keep[:], in0=tot[:, :, 0:2], scalar1=0.5, scalar2=None, op0=ALU.is_gt
-            )
-
-            words = a_raw[:].bitcast(F32).rearrange("p (c w u) -> p c u w", c=PASSES, u=2)
-            grouped = awork.tile([P, PACK * K_PASS], BF16, name="a_grouped", tag="a_grouped", align_bytes=64)
-            grouped_w = grouped[:].bitcast(F32).rearrange("p (c m u) -> p c m u", c=PASSES, u=2)
+        def transpose_a(g):
+            words = a_raw[g][:].bitcast(F32).rearrange("p (c w u) -> p c u w", c=PASSES, u=2)
+            a_grp[g] = agrp_pool.tile([P, PACK * K_PASS], BF16, name="a_grp", tag="a_grp", align_bytes=64)
+            grouped_w = a_grp[g][:].bitcast(F32).rearrange("p (c m u) -> p c m u", c=PASSES, u=2)
             for h in range(2):
                 xt = psum.tile([P, 2, 2, P], F32, name="xt", tag="bank")
                 for ci in range(2):
@@ -112,78 +85,200 @@ def tile_sparsebmm_kernel(tc, a, b, out):
                     out=grouped_w[:, 2 * h : 2 * h + 2],
                     in_=xt[:].rearrange("p c u m -> p c m u"),
                 )
-            by_tile = grouped[:].rearrange("p (t e) -> p t e", e=256)
-            nc.vector.tensor_tensor(
-                out=by_tile,
-                in0=by_tile,
-                in1=keep[:].rearrange("p c j -> p (c j)").unsqueeze(2).to_broadcast([P, 8, 256]),
-                op=ALU.mult,
+
+        def magnitude(g):
+            big[g] = awork.tile([P, K], BF16, name="big", tag="big")
+            nc.vector.tensor_scalar(
+                out=big[g][:].bitcast(I32),
+                in0=a_raw[g][:].bitcast(I32),
+                scalar1=0x7FFF7FFF,
+                scalar2=None,
+                op0=ALU.bitwise_and,
             )
+
+        def flag_big(g):
+            nc.vector.tensor_scalar(
+                out=big[g][:], in0=big[g][:], scalar1=THRESHOLD, scalar2=None, op0=ALU.is_gt
+            )
+
+        def count_columns(g):
+            cnt[g] = psum.tile([P, 16, 32], F32, name="cnt", tag="bank")
+            for kc in range(16):
+                nc.tensor.matmul(
+                    out=cnt[g][:, kc, :],
+                    lhsT=big[g][:, kc * P : (kc + 1) * P],
+                    rhs=sel[:],
+                    start=True,
+                    stop=True,
+                )
+
+        def count_tiles(g):
+            cnt_sb = awork.tile([P, 16, 8], BF16, name="cnt_sb", tag="cnt_sb", bufs=3)
+            nc.vector.tensor_copy(out=cnt_sb[:], in_=cnt[g][:, :, 0:8])
+            tot[g] = psum.tile([P, PASSES, 8], F32, name="tot", tag="bank")
+            cnt_by_q = cnt_sb[:].rearrange("p (c q) e -> p q c e", q=4)
+            for q in range(4):
+                nc.tensor.matmul(
+                    out=tot[g][:],
+                    lhsT=spread[:, q, :],
+                    rhs=cnt_by_q[:, q],
+                    start=(q == 0),
+                    stop=(q == 3),
+                )
+
+        def make_keep(g):
+            keep[g] = keep_pool.tile([P, PASSES, 2], F32, name="keep", tag="keep")
+            nc.vector.tensor_scalar(
+                out=keep[g][:], in0=tot[g][:, :, 0:2], scalar1=0.5, scalar2=None, op0=ALU.is_gt
+            )
+
+        def mask_a(g):
+            for c in range(PASSES):
+                for j in range(2):
+                    part = a_grp[g][:, (2 * c + j) * 256 : (2 * c + j + 1) * 256]
+                    nc.vector.tensor_scalar(
+                        out=part, in0=part, scalar1=keep[g][:, c, j : j + 1], scalar2=None, op0=ALU.mult
+                    )
+
+        def quantise_a(g):
             nc.vector.quantize_mx(
                 out=a_codes[:, g, :].bitcast(FP8X4),
                 scales=a_scales[:, g, :],
-                in_=grouped[:],
+                in_=a_grp[g][:],
             )
 
-        chunk = 0
-        for bi in range(B):
-            for nh in range(N // N_HALF):
-                last_round = bi == B - 1 and nh == N // N_HALF - 1
-                cols = slice(nh * N_HALF, (nh + 1) * N_HALF)
+        def width(i):
+            return ROUNDS[i // PASSES][2]
+
+        def load_b(i):
+            if i >= n_chunks:
+                return
+            bi, n0, w = ROUNDS[i // PASSES]
+            c = i % PASSES
+            b_raw[i] = braw_pool.tile([P, PACK, w], BF16, name="b_raw", tag="b_raw")
+            nc.sync.dma_start(
+                out=b_raw[i][:],
+                in_=b[bi, c * K_PASS : (c + 1) * K_PASS, n0 : n0 + w].rearrange("(p t) n -> p t n", t=PACK),
+            )
+
+        def grouped_b(i):
+            if i not in b_grp:
+                b_grp[i] = bgrp_pool.tile([P, width(i), PACK], BF16, name="b_grp", tag="b_grp", align_bytes=64)
+            return b_grp[i]
+
+        def regroup(engine_copy, i, lo, hi):
+            engine_copy(
+                out=grouped_b(i)[:, lo:hi, :].rearrange("p (c i) t -> p c t i", i=4),
+                in_=b_raw[i][:, :, lo:hi].rearrange("p t (c i) -> p c t i", i=4),
+            )
+
+        def scalar_up_to(n):
+            for i in range(done["rs"], min(n, n_chunks)):
+                for lo in range(width(i) - S_COLS[i], width(i), S_PIECE):
+                    regroup(nc.scalar.copy, i, lo, min(lo + S_PIECE, width(i)))
+                done["rs"] = i + 1
+
+        def vector_up_to(n):
+            for i in range(done["rv"], min(n, n_chunks)):
+                if S_COLS[i] < width(i):
+                    regroup(nc.vector.tensor_copy, i, 0, width(i) - S_COLS[i])
+                done["rv"] = i + 1
+
+        def quantise_up_to(n):
+            for i in range(done["q"], min(n, n_chunks)):
+                scalar_up_to(i + 1)
+                vector_up_to(i + 1)
+                w = width(i)
+                codes = bq_pool.tile([P, w], U32, name="b_codes", tag="b_codes", align_bytes=64)
+                scales = bq_pool.tile([P, w], U8, name="b_scales", tag="b_scales", align_bytes=64)
+                nc.vector.quantize_mx(
+                    out=codes[:].bitcast(FP8X4),
+                    scales=scales[:],
+                    in_=b_grp[i][:].rearrange("p n t -> p (n t)"),
+                )
+                b_q[i] = (codes, scales)
+                load_b(i + B_RAW_BUFS)
+                done["q"] = i + 1
+
+        for g in range(M_TILES):
+            load_a(g)
+        load_b(0)
+        load_b(1)
+        n_a = B * M_TILES
+        for s in range(n_a + 3):
+            if s < n_a:
+                transpose_a(s)
+                magnitude(s)
+            if 3 <= s < 3 + M_TILES:
+                mask_a(s - 3)
+            if 1 <= s <= n_a:
+                count_tiles(s - 1)
+            if 3 <= s < 3 + M_TILES:
+                quantise_a(s - 3)
+            if s < n_a:
+                flag_big(s)
+                count_columns(s)
+                if s < M_TILES:
+                    load_a(s + M_TILES)
+                if s == M_TILES - 1:
+                    for i in range(2, B_RAW_BUFS):
+                        load_b(i)
+            if 2 <= s <= n_a + 1:
+                make_keep(s - 2)
+            if s == 3:
+                scalar_up_to(1)
+            if s == 5:
+                scalar_up_to(2)
+            if s == 7:
+                vector_up_to(1)
+            if s == 8:
+                vector_up_to(2)
+                quantise_up_to(1)
+            if s == 9:
+                vector_up_to(3)
+                quantise_up_to(2)
+
+        accs = []
+        for i in range(n_chunks):
+            r, c = divmod(i, PASSES)
+            bi, n0, w = ROUNDS[r]
+            n_tiles = w // N_TILE
+            scalar_up_to(i + 1 + S_AHEAD)
+            if i < M_TILES:
+                mask_a(M_TILES + i)
+            vector_up_to(i + 1 + V_AHEAD)
+            if i < M_TILES:
+                quantise_a(M_TILES + i)
+            quantise_up_to(i + 1 + Q_AHEAD)
+            if c == 0:
                 accs = []
-                for i in range(M_TILES * 2):
+                for k in range(M_TILES * n_tiles):
                     acc = psum.tile([P, N_TILE], F32, name="acc", tag="bank")
                     accs.append(acc)
-                for c in range(PASSES):
-                    b_raw = braw_pool.tile([P, PACK, N_HALF], BF16, name="b_raw", tag="b_raw")
-                    nc.sync.dma_start(
-                        out=b_raw[:],
-                        in_=b[bi, c * K_PASS : (c + 1) * K_PASS, cols].rearrange(
-                            "(p t) n -> p t n", t=PACK
-                        ),
+            codes, scales = b_q[i]
+            for mt in range(M_TILES):
+                g = bi * M_TILES + mt
+                for nt in range(n_tiles):
+                    nc.tensor.matmul_mx(
+                        out=accs[n_tiles * mt + nt][:],
+                        lhsT=a_codes[:, g, c * P : (c + 1) * P].bitcast(FP8X4),
+                        lhsT_scale=a_scales[:, g, c * P : (c + 1) * P],
+                        rhs=codes[:, nt * N_TILE : (nt + 1) * N_TILE].bitcast(FP8X4),
+                        rhs_scale=scales[:, nt * N_TILE : (nt + 1) * N_TILE],
+                        start=(c == 0),
+                        stop=(c == PASSES - 1),
                     )
-                    b_grp = bgrp_pool.tile([P, N_HALF, PACK], BF16, name="b_grp", tag="b_grp", align_bytes=64)
-                    s_cols = S_COLS_FIRST if chunk < FIRST_CHUNKS else S_COLS
-                    v_cols = N_HALF - s_cols
-                    if v_cols > 0:
-                        nc.vector.tensor_copy(
-                            out=b_grp[:, 0:v_cols, :].rearrange("p (c i) t -> p c t i", i=4),
-                            in_=b_raw[:, :, 0:v_cols].rearrange("p t (c i) -> p c t i", i=4),
-                        )
-                    nc.scalar.copy(
-                        out=b_grp[:, v_cols:N_HALF, :].rearrange("p (c i) t -> p c t i", i=4),
-                        in_=b_raw[:, :, v_cols:N_HALF].rearrange("p t (c i) -> p c t i", i=4),
-                    )
-                    b_codes = bq_pool.tile([P, N_HALF], U32, name="b_codes", tag="b_codes", align_bytes=64)
-                    b_scales = bq_pool.tile([P, N_HALF], U8, name="b_scales", tag="b_scales", align_bytes=64)
-                    nc.vector.quantize_mx(
-                        out=b_codes[:].bitcast(FP8X4),
-                        scales=b_scales[:],
-                        in_=b_grp[:].rearrange("p n t -> p (n t)"),
-                    )
-                    for mt in range(M_TILES):
-                        g = bi * M_TILES + mt
-                        for nt in range(2):
-                            nc.tensor.matmul_mx(
-                                out=accs[2 * mt + nt][:],
-                                lhsT=a_codes[:, g, c * P : (c + 1) * P].bitcast(FP8X4),
-                                lhsT_scale=a_scales[:, g, c * P : (c + 1) * P],
-                                rhs=b_codes[:, nt * N_TILE : (nt + 1) * N_TILE].bitcast(FP8X4),
-                                rhs_scale=b_scales[:, nt * N_TILE : (nt + 1) * N_TILE],
-                                start=(c == 0),
-                                stop=(c == PASSES - 1),
-                            )
-                    chunk += 1
+            if c == PASSES - 1:
                 for mt in range(M_TILES):
-                    stage = stage_pool.tile([P, N_HALF], F32, name="stage", tag="stage")
-                    on_vector = last_round and mt % 2 == 1
-                    for nt in range(2):
+                    on_vector = r == len(ROUNDS) - 1 and mt % 2 == 1
+                    stage = stage_pool.tile([P, w], F32, name="stage", tag="stage")
+                    for nt in range(n_tiles):
                         dst = stage[:, nt * N_TILE : (nt + 1) * N_TILE]
                         if on_vector:
-                            nc.vector.tensor_copy(out=dst, in_=accs[2 * mt + nt][:])
+                            nc.vector.tensor_copy(out=dst, in_=accs[n_tiles * mt + nt][:])
                         else:
-                            nc.scalar.copy(out=dst, in_=accs[2 * mt + nt][:])
-                    rows = out[bi, mt * P : (mt + 1) * P, cols]
+                            nc.scalar.copy(out=dst, in_=accs[n_tiles * mt + nt][:])
+                    rows = out[bi, mt * P : (mt + 1) * P, n0 : n0 + w]
                     if on_vector:
                         nc.sync.dma_start(out=rows, in_=stage[:])
                     else:

@@ -28,7 +28,7 @@ B_RAW_BUFS = 8
 S_AHEAD = 3
 V_AHEAD = 2
 Q_AHEAD = 1
-PIN = True
+PIN = False
 
 
 def tile_sparsebmm_kernel(tc, a, b, out):

@@ -24,7 +24,8 @@ FLOPS = 2 * B * M * K * N
 ROUNDS = ((0, 0, 1024), (0, 1024, 1024), (1, 0, 1024), (1, 1024, 512), (1, 1536, 512))
 S_COLS = (640, 1024, 640, 640, 384, 320, 320, 576, 384, 320, 320, 576, 288, 288, 0, 0, 160, 160, 96, 96)
 S_PIECE = 512
-B_RAW_BUFS = 8
+N_B0 = 8
+RAW_BYTES = PACK * 1024 * 2
 S_AHEAD = 3
 V_AHEAD = 2
 Q_AHEAD = 1
@@ -40,7 +41,7 @@ def tile_sparsebmm_kernel(tc, a, b, out):
         awork = ctx.enter_context(tc.tile_pool(name="awork", bufs=2))
         agrp_pool = ctx.enter_context(tc.tile_pool(name="agrp", bufs=6))
         keep_pool = ctx.enter_context(tc.tile_pool(name="keep", bufs=8))
-        braw_pool = ctx.enter_context(tc.tile_pool(name="braw", bufs=B_RAW_BUFS))
+        braw_pool = ctx.enter_context(tc.tile_pool(name="braw", bufs=1))
         bgrp_pool = ctx.enter_context(tc.tile_pool(name="bgrp", bufs=5))
         bq_pool = ctx.enter_context(tc.tile_pool(name="bq", bufs=6))
         stage_pool = ctx.enter_context(tc.tile_pool(name="stage", bufs=4))
@@ -151,15 +152,24 @@ def tile_sparsebmm_kernel(tc, a, b, out):
             return ROUNDS[i // PASSES][2]
 
         def load_b(i):
-            if i >= n_chunks:
-                return
             bi, n0, w = ROUNDS[i // PASSES]
             c = i % PASSES
-            b_raw[i] = braw_pool.tile([P, PACK, w], BF16, name="b_raw", tag="b_raw")
+            raw = braw_pool.tile([P, PACK, w], BF16, name="b_raw%d" % i, offset=i * RAW_BYTES)
             nc.sync.dma_start(
-                out=b_raw[i][:],
+                out=raw[:],
                 in_=b[bi, c * K_PASS : (c + 1) * K_PASS, n0 : n0 + w].rearrange("(p t) n -> p t n", t=PACK),
             )
+            b_raw[i] = raw[:]
+
+        def load_slab(c):
+            slab = braw_pool.tile([P, PACK, N], BF16, name="b_slab%d" % c, offset=2 * c * RAW_BYTES)
+            nc.sync.dma_start(
+                out=slab[:],
+                in_=b[1, c * K_PASS : (c + 1) * K_PASS, :].rearrange("(p t) n -> p t n", t=PACK),
+            )
+            for r in range(N_B0 // PASSES, len(ROUNDS)):
+                n0, w = ROUNDS[r][1], ROUNDS[r][2]
+                b_raw[r * PASSES + c] = slab[:, :, n0 : n0 + w]
 
         def grouped_b(i):
             if i not in b_grp:
@@ -197,7 +207,8 @@ def tile_sparsebmm_kernel(tc, a, b, out):
                     in_=b_grp[i][:].rearrange("p n t -> p (n t)"),
                 )
                 b_q[i] = (codes, scales)
-                load_b(i + B_RAW_BUFS)
+                if i < N_B0 and i % 2 == 1:
+                    load_slab(i // 2)
                 done["q"] = i + 1
 
         for g in range(M_TILES):
@@ -221,7 +232,7 @@ def tile_sparsebmm_kernel(tc, a, b, out):
                 if s < M_TILES:
                     load_a(s + M_TILES)
                 if s == M_TILES - 1:
-                    for i in range(2, B_RAW_BUFS):
+                    for i in range(2, N_B0):
                         load_b(i)
             if 2 <= s <= n_a + 1:
                 make_keep(s - 2)

@@ -37,7 +37,7 @@ def tile_sparsebmm_kernel(tc, a, b, out):
     n_chunks = len(ROUNDS) * PASSES
     with ExitStack() as ctx:
         const = ctx.enter_context(tc.tile_pool(name="const", bufs=1))
-        araw_pool = ctx.enter_context(tc.tile_pool(name="araw", bufs=4))
+        araw_pool = ctx.enter_context(tc.tile_pool(name="araw", bufs=8))
         awork = ctx.enter_context(tc.tile_pool(name="awork", bufs=2))
         agrp_pool = ctx.enter_context(tc.tile_pool(name="agrp", bufs=6))
         keep_pool = ctx.enter_context(tc.tile_pool(name="keep", bufs=8))
@@ -211,43 +211,37 @@ def tile_sparsebmm_kernel(tc, a, b, out):
                     load_slab(i // 2)
                 done["q"] = i + 1
 
-        for g in range(M_TILES):
-            load_a(g)
-        load_b(0)
-        load_b(1)
         n_a = B * M_TILES
-        for s in range(n_a + 3):
-            if s < n_a:
-                transpose_a(s)
-                magnitude(s)
-            if 3 <= s < 3 + M_TILES:
-                mask_a(s - 3)
-            if 1 <= s <= n_a:
-                count_tiles(s - 1)
-            if 3 <= s < 3 + M_TILES:
-                quantise_a(s - 3)
-            if s < n_a:
-                flag_big(s)
-                count_columns(s)
-                if s < M_TILES:
-                    load_a(s + M_TILES)
-                if s == M_TILES - 1:
-                    for i in range(2, N_B0):
-                        load_b(i)
-            if 2 <= s <= n_a + 1:
-                make_keep(s - 2)
-            if s == 3:
-                scalar_up_to(1)
-            if s == 5:
-                scalar_up_to(2)
-            if s == 7:
-                vector_up_to(1)
-            if s == 8:
-                vector_up_to(2)
-                quantise_up_to(1)
-            if s == 9:
-                vector_up_to(3)
-                quantise_up_to(2)
+        with tc.manual_schedule(engines={mybir.EngineType.Activation, mybir.EngineType.SP}):
+            for g in range(n_a):
+                load_a(g)
+            for i in range(N_B0):
+                load_b(i)
+            for s in range(n_a + 3):
+                if s < n_a:
+                    transpose_a(s)
+                    magnitude(s)
+                if 3 <= s < 3 + M_TILES:
+                    mask_a(s - 3)
+                if 1 <= s <= n_a:
+                    count_tiles(s - 1)
+                if 3 <= s < 3 + M_TILES:
+                    quantise_a(s - 3)
+                if s < n_a:
+                    flag_big(s)
+                    count_columns(s)
+                if 2 <= s <= n_a + 1:
+                    make_keep(s - 2)
+                if s == 7:
+                    scalar_up_to(1)
+                    vector_up_to(1)
+                if s == 8:
+                    scalar_up_to(2)
+                    vector_up_to(2)
+                    quantise_up_to(1)
+                if s == 9:
+                    vector_up_to(3)
+                    quantise_up_to(2)
 
         accs = []
         for i in range(n_chunks):

@@ -22,7 +22,7 @@ N_TILE = 512
 FLOPS = 2 * B * M * K * N
 
 ROUNDS = ((0, 0, 1024), (0, 1024, 1024), (1, 0, 1024), (1, 1024, 512), (1, 1536, 512))
-S_COLS = (640, 1024, 640, 640, 384, 320, 320, 576, 384, 320, 320, 576, 288, 288, 0, 0, 160, 160, 96, 96)
+S_COLS = (640, 1024, 640, 640, 256, 192, 192, 448, 256, 192, 192, 448, 288, 288, 0, 0, 160, 160, 96, 96)
 S_PIECE = 512
 N_B0 = 8
 RAW_BYTES = PACK * 1024 * 2
@@ -284,7 +284,4 @@ def tile_sparsebmm_kernel(tc, a, b, out):
                         else:
                             nc.scalar.copy(out=dst, in_=accs[n_tiles * mt + nt][:])
                     rows = out[bi, mt * P : (mt + 1) * P, n0 : n0 + w]
-                    if on_vector:
-                        nc.sync.dma_start(out=rows, in_=stage[:])
-                    else:
-                        nc.scalar.dma_start(out=rows, in_=stage[:])
+                    nc.sync.dma_start(out=rows, in_=stage[:])

@@ -22,7 +22,7 @@ N_TILE = 512
 FLOPS = 2 * B * M * K * N
 
 ROUNDS = ((0, 0, 1024), (0, 1024, 1024), (1, 0, 1024), (1, 1024, 512), (1, 1536, 512))
-S_COLS = (640, 1024, 640, 640, 256, 192, 192, 448, 256, 192, 192, 448, 288, 288, 0, 0, 160, 160, 96, 96)
+S_COLS = (640, 1024, 640, 640, 384, 320, 320, 512, 256, 192, 192, 448, 288, 288, 0, 0, 160, 160, 96, 96)
 S_PIECE = 512
 N_B0 = 8
 RAW_BYTES = PACK * 1024 * 2
@@ -30,6 +30,7 @@ S_AHEAD = 3
 V_AHEAD = 2
 Q_AHEAD = 1
 PIN = False
+LAG = 2
 
 
 def tile_sparsebmm_kernel(tc, a, b, out):
@@ -243,29 +244,23 @@ def tile_sparsebmm_kernel(tc, a, b, out):
                     vector_up_to(3)
                     quantise_up_to(2)
 
-        accs = []
-        for i in range(n_chunks):
+        accs = {}
+
+        def multiply(i, m_tiles):
             r, c = divmod(i, PASSES)
             bi, n0, w = ROUNDS[r]
             n_tiles = w // N_TILE
-            scalar_up_to(i + 1 + S_AHEAD)
-            if i < M_TILES:
-                mask_a(M_TILES + i)
-            vector_up_to(i + 1 + V_AHEAD)
-            if i < M_TILES:
-                quantise_a(M_TILES + i)
-            quantise_up_to(i + 1 + Q_AHEAD)
             if c == 0:
-                accs = []
-                for k in range(M_TILES * n_tiles):
-                    acc = psum.tile([P, N_TILE], F32, name="acc", tag="bank")
-                    accs.append(acc)
+                for mt in m_tiles:
+                    for nt in range(n_tiles):
+                        acc = psum.tile([P, N_TILE], F32, name="acc", tag="bank")
+                        accs[(r, mt, nt)] = acc
             codes, scales = b_q[i]
-            for mt in range(M_TILES):
+            for mt in m_tiles:
                 g = bi * M_TILES + mt
                 for nt in range(n_tiles):
                     nc.tensor.matmul_mx(
-                        out=accs[n_tiles * mt + nt][:],
+                        out=accs[(r, mt, nt)][:],
                         lhsT=a_codes[:, g, c * P : (c + 1) * P].bitcast(FP8X4),
                         lhsT_scale=a_scales[:, g, c * P : (c + 1) * P],
                         rhs=codes[:, nt * N_TILE : (nt + 1) * N_TILE].bitcast(FP8X4),
@@ -274,14 +269,32 @@ def tile_sparsebmm_kernel(tc, a, b, out):
                         stop=(c == PASSES - 1),
                     )
             if c == PASSES - 1:
-                for mt in range(M_TILES):
+                for mt in m_tiles:
                     on_vector = r == len(ROUNDS) - 1 and mt % 2 == 1
                     stage = stage_pool.tile([P, w], F32, name="stage", tag="stage")
                     for nt in range(n_tiles):
                         dst = stage[:, nt * N_TILE : (nt + 1) * N_TILE]
                         if on_vector:
-                            nc.vector.tensor_copy(out=dst, in_=accs[n_tiles * mt + nt][:])
+                            nc.vector.tensor_copy(out=dst, in_=accs[(r, mt, nt)][:])
                         else:
-                            nc.scalar.copy(out=dst, in_=accs[n_tiles * mt + nt][:])
+                            nc.scalar.copy(out=dst, in_=accs[(r, mt, nt)][:])
                     rows = out[bi, mt * P : (mt + 1) * P, n0 : n0 + w]
                     nc.sync.dma_start(out=rows, in_=stage[:])
+
+        def wide(i):
+            return 0 <= i < n_chunks and width(i) == 2 * N_TILE
+
+        for i in range(n_chunks):
+            scalar_up_to(i + 1 + S_AHEAD)
+            if i < M_TILES:
+                mask_a(M_TILES + i)
+            vector_up_to(i + 1 + V_AHEAD)
+            if i < M_TILES:
+                quantise_a(M_TILES + i)
+            quantise_up_to(i + 1 + Q_AHEAD)
+            if wide(i - LAG):
+                multiply(i - LAG, (2, 3))
+            if wide(i):
+                multiply(i, (0, 1))
+            else:
+                multiply(i, (0, 1, 2, 3))

@@ -22,7 +22,7 @@ N_TILE = 512
 FLOPS = 2 * B * M * K * N
 
 ROUNDS = ((0, 0, 1024), (0, 1024, 1024), (1, 0, 1024), (1, 1024, 512), (1, 1536, 512))
-S_COLS = (640, 1024, 640, 640, 384, 320, 320, 512, 256, 192, 192, 448, 288, 288, 0, 0, 160, 160, 96, 96)
+S_COLS = (576, 896, 576, 576, 384, 320, 320, 512, 256, 192, 192, 448, 288, 288, 0, 0, 160, 160, 96, 96)
 S_PIECE = 512
 N_B0 = 8
 RAW_BYTES = PACK * 1024 * 2

@@ -115,9 +115,9 @@ def tile_sparsebmm_kernel(tc, a, b, out):
                 )
 
         def count_tiles(g):
-            cnt_sb = awork.tile([P, 16, 8], BF16, name="cnt_sb", tag="cnt_sb", bufs=3)
-            nc.vector.tensor_copy(out=cnt_sb[:], in_=cnt[g][:, :, 0:8])
-            tot[g] = psum.tile([P, PASSES, 8], F32, name="tot", tag="bank")
+            cnt_sb = awork.tile([P, 16, 2], BF16, name="cnt_sb", tag="cnt_sb", bufs=3)
+            nc.vector.tensor_copy(out=cnt_sb[:], in_=cnt[g][:, :, 0:2])
+            tot[g] = psum.tile([P, PASSES, 2], F32, name="tot", tag="bank")
             cnt_by_q = cnt_sb[:].rearrange("p (c q) e -> p q c e", q=4)
             for q in range(4):
                 nc.tensor.matmul(
@@ -131,7 +131,7 @@ def tile_sparsebmm_kernel(tc, a, b, out):
         def make_keep(g):
             keep[g] = keep_pool.tile([P, PASSES, 2], F32, name="keep", tag="keep")
             nc.vector.tensor_scalar(
-                out=keep[g][:], in0=tot[g][:, :, 0:2], scalar1=0.5, scalar2=None, op0=ALU.is_gt
+                out=keep[g][:], in0=tot[g][:], scalar1=0.5, scalar2=None, op0=ALU.is_gt
             )
 
         def mask_a(g):

@@ -40,12 +40,11 @@ def tile_sparsebmm_kernel(tc, a, b, out):
         const = ctx.enter_context(tc.tile_pool(name="const", bufs=1))
         araw_pool = ctx.enter_context(tc.tile_pool(name="araw", bufs=8))
         awork = ctx.enter_context(tc.tile_pool(name="awork", bufs=2))
-        agrp_pool = ctx.enter_context(tc.tile_pool(name="agrp", bufs=6))
+        agrp_pool = ctx.enter_context(tc.tile_pool(name="agrp", bufs=8))
         keep_pool = ctx.enter_context(tc.tile_pool(name="keep", bufs=8))
         braw_pool = ctx.enter_context(tc.tile_pool(name="braw", bufs=1))
         bgrp_pool = ctx.enter_context(tc.tile_pool(name="bgrp", bufs=5))
         bq_pool = ctx.enter_context(tc.tile_pool(name="bq", bufs=6))
-        stage_pool = ctx.enter_context(tc.tile_pool(name="stage", bufs=4))
         psum = ctx.enter_context(tc.psum_pool(name="psum", bufs=8))
         if PIN:
             ctx.enter_context(tc.manual_schedule())
@@ -271,7 +270,7 @@ def tile_sparsebmm_kernel(tc, a, b, out):
             if c == PASSES - 1:
                 for mt in m_tiles:
                     on_vector = r == len(ROUNDS) - 1 and mt % 2 == 1
-                    stage = stage_pool.tile([P, w], F32, name="stage", tag="stage")
+                    stage = agrp_pool.tile([P, w], F32, name="stage", tag="a_grp", align_bytes=64)
                     for nt in range(n_tiles):
                         dst = stage[:, nt * N_TILE : (nt + 1) * N_TILE]
                         if on_vector:

@@ -22,14 +22,14 @@ N_TILE = 512
 FLOPS = 2 * B * M * K * N
 
 ROUNDS = ((0, 0, 1024), (0, 1024, 1024), (1, 0, 1024), (1, 1024, 512), (1, 1536, 512))
-S_COLS = (576, 896, 576, 576, 384, 320, 320, 512, 256, 192, 192, 448, 288, 288, 0, 0, 160, 160, 96, 96)
+S_COLS = (768, 384, 352, 160, 160)
 S_PIECE = 512
 N_B0 = 8
 RAW_BYTES = PACK * 1024 * 2
+T_AHEAD = 3
 S_AHEAD = 3
 V_AHEAD = 2
 Q_AHEAD = 1
-PIN = False
 LAG = 2
 
 
@@ -39,15 +39,13 @@ def tile_sparsebmm_kernel(tc, a, b, out):
     with ExitStack() as ctx:
         const = ctx.enter_context(tc.tile_pool(name="const", bufs=1))
         araw_pool = ctx.enter_context(tc.tile_pool(name="araw", bufs=8))
-        awork = ctx.enter_context(tc.tile_pool(name="awork", bufs=2))
+        awork = ctx.enter_context(tc.tile_pool(name="awork", bufs=4))
         agrp_pool = ctx.enter_context(tc.tile_pool(name="agrp", bufs=8))
         keep_pool = ctx.enter_context(tc.tile_pool(name="keep", bufs=8))
         braw_pool = ctx.enter_context(tc.tile_pool(name="braw", bufs=1))
         bgrp_pool = ctx.enter_context(tc.tile_pool(name="bgrp", bufs=5))
         bq_pool = ctx.enter_context(tc.tile_pool(name="bq", bufs=6))
         psum = ctx.enter_context(tc.psum_pool(name="psum", bufs=8))
-        if PIN:
-            ctx.enter_context(tc.manual_schedule())
 
         ident = const.tile([P, P], F32, name="ident")
         make_identity(nc, ident[:])
@@ -151,6 +149,9 @@ def tile_sparsebmm_kernel(tc, a, b, out):
         def width(i):
             return ROUNDS[i // PASSES][2]
 
+        def s_cols(i):
+            return S_COLS[i // PASSES] if i else width(i)
+
         def load_b(i):
             bi, n0, w = ROUNDS[i // PASSES]
             c = i % PASSES
@@ -184,14 +185,14 @@ def tile_sparsebmm_kernel(tc, a, b, out):
 
         def scalar_up_to(n):
             for i in range(done["rs"], min(n, n_chunks)):
-                for lo in range(width(i) - S_COLS[i], width(i), S_PIECE):
+                for lo in range(width(i) - s_cols(i), width(i), S_PIECE):
                     regroup(nc.scalar.copy, i, lo, min(lo + S_PIECE, width(i)))
                 done["rs"] = i + 1
 
         def vector_up_to(n):
             for i in range(done["rv"], min(n, n_chunks)):
-                if S_COLS[i] < width(i):
-                    regroup(nc.vector.tensor_copy, i, 0, width(i) - S_COLS[i])
+                if s_cols(i) < width(i):
+                    regroup(nc.vector.tensor_copy, i, 0, width(i) - s_cols(i))
                 done["rv"] = i + 1
 
         def quantise_up_to(n):
@@ -212,36 +213,30 @@ def tile_sparsebmm_kernel(tc, a, b, out):
                 done["q"] = i + 1
 
         n_a = B * M_TILES
-        with tc.manual_schedule(engines={mybir.EngineType.Activation, mybir.EngineType.SP}):
+        with tc.manual_schedule():
             for g in range(n_a):
                 load_a(g)
             for i in range(N_B0):
                 load_b(i)
-            for s in range(n_a + 3):
+            for g in range(T_AHEAD):
+                transpose_a(g)
+            for s in range(n_a + 4):
                 if s < n_a:
-                    transpose_a(s)
                     magnitude(s)
-                if 3 <= s < 3 + M_TILES:
-                    mask_a(s - 3)
                 if 1 <= s <= n_a:
-                    count_tiles(s - 1)
-                if 3 <= s < 3 + M_TILES:
-                    quantise_a(s - 3)
-                if s < n_a:
-                    flag_big(s)
-                    count_columns(s)
-                if 2 <= s <= n_a + 1:
-                    make_keep(s - 2)
-                if s == 7:
-                    scalar_up_to(1)
-                    vector_up_to(1)
-                if s == 8:
-                    scalar_up_to(2)
-                    vector_up_to(2)
-                    quantise_up_to(1)
-                if s == 9:
-                    vector_up_to(3)
-                    quantise_up_to(2)
+                    flag_big(s - 1)
+                    count_columns(s - 1)
+                if 3 <= s <= n_a + 2:
+                    count_tiles(s - 3)
+                if 4 <= s:
+                    make_keep(s - 4)
+                if n_a <= s:
+                    mask_a(s - n_a)
+                if n_a + 2 <= s:
+                    quantise_a(s - n_a - 2)
+                if 1 <= s and s + T_AHEAD - 1 < n_a:
+                    transpose_a(s + T_AHEAD - 1)
+            scalar_up_to(2)
 
         accs = {}
 
@@ -285,6 +280,9 @@ def tile_sparsebmm_kernel(tc, a, b, out):
 
         for i in range(n_chunks):
             scalar_up_to(i + 1 + S_AHEAD)
+            if i == 0:
+                quantise_a(M_TILES - 2)
+                quantise_a(M_TILES - 1)
             if i < M_TILES:
                 mask_a(M_TILES + i)
             vector_up_to(i + 1 + V_AHEAD)

@@ -10,6 +10,7 @@ U32 = mybir.dt.uint32
 U8 = mybir.dt.uint8
 FP8X4 = mybir.dt.float8_e4m3fn_x4
 ALU = mybir.AluOpType
+ACT = mybir.ActivationFunctionType
 
 B, M, K, N = 2, 512, 2048, 2048
 THRESHOLD = 1e-6
@@ -22,11 +23,12 @@ N_TILE = 512
 FLOPS = 2 * B * M * K * N
 
 ROUNDS = ((0, 0, 1024), (0, 1024, 1024), (1, 0, 1024), (1, 1024, 512), (1, 1536, 512))
-S_COLS = (768, 384, 352, 160, 160)
+S_COLS = (704, 448, 416, 160, 96)
 S_PIECE = 512
 N_B0 = 8
 RAW_BYTES = PACK * 1024 * 2
-T_AHEAD = 3
+A_BYTES = N_B0 * RAW_BYTES
+SLAB_BEHIND = (1, 3, 4, 5)
 S_AHEAD = 3
 V_AHEAD = 2
 Q_AHEAD = 1
@@ -38,21 +40,24 @@ def tile_sparsebmm_kernel(tc, a, b, out):
     n_chunks = len(ROUNDS) * PASSES
     with ExitStack() as ctx:
         const = ctx.enter_context(tc.tile_pool(name="const", bufs=1))
-        araw_pool = ctx.enter_context(tc.tile_pool(name="araw", bufs=8))
         awork = ctx.enter_context(tc.tile_pool(name="awork", bufs=4))
         agrp_pool = ctx.enter_context(tc.tile_pool(name="agrp", bufs=8))
-        keep_pool = ctx.enter_context(tc.tile_pool(name="keep", bufs=8))
-        braw_pool = ctx.enter_context(tc.tile_pool(name="braw", bufs=1))
+        keep_pool = ctx.enter_context(tc.tile_pool(name="keep", bufs=2))
+        raw_pool = ctx.enter_context(tc.tile_pool(name="raw", bufs=1))
         bgrp_pool = ctx.enter_context(tc.tile_pool(name="bgrp", bufs=5))
         bq_pool = ctx.enter_context(tc.tile_pool(name="bq", bufs=6))
         psum = ctx.enter_context(tc.psum_pool(name="psum", bufs=8))
 
         ident = const.tile([P, P], F32, name="ident")
         make_identity(nc, ident[:])
-        sel = const.tile([P, 32], BF16, name="sel")
-        nc.gpsimd.memset(sel[:], 0.0)
-        nc.gpsimd.memset(sel[0:64, 0:1], 1.0)
-        nc.gpsimd.memset(sel[64:128, 1:2], 1.0)
+        halves = const.tile([P, 2], BF16, name="halves")
+        nc.gpsimd.memset(halves[:], 0.0)
+        nc.gpsimd.memset(halves[0:64, 0:1], 1.0)
+        nc.gpsimd.memset(halves[64:128, 1:2], 1.0)
+        one = const.tile([P, 1], F32, name="one")
+        nc.gpsimd.memset(one[:], 1.0)
+        sel = const.tile([P, 2], BF16, name="sel")
+        nc.scalar.activation(out=sel[:].bitcast(F32), in_=halves[:].bitcast(F32), func=ACT.Copy, scale=one[:])
         spread = const.tile([P, 4, P], BF16, name="spread")
         nc.gpsimd.memset(spread[:], 0.0)
         for q in range(4):
@@ -62,28 +67,36 @@ def tile_sparsebmm_kernel(tc, a, b, out):
         a_codes = const.tile([P, B * M_TILES, K_PASS], U32, name="a_codes", align_bytes=64)
         a_scales = const.tile([P, B * M_TILES, K_PASS], U8, name="a_scales", align_bytes=64)
 
-        a_raw, big, a_grp, cnt, tot, keep = {}, {}, {}, {}, {}, {}
+        a_raw, big, xt, a_grp, cnt, tot, keep = {}, {}, {}, {}, {}, {}, {}
         b_raw, b_grp, b_q = {}, {}, {}
         done = {"rs": 0, "rv": 0, "q": 0}
 
         def load_a(g):
             bi, mt = divmod(g, M_TILES)
-            a_raw[g] = araw_pool.tile([P, K], BF16, name="a_raw", tag="a_raw")
+            a_raw[g] = raw_pool.tile([P, K], BF16, name="a_raw%d" % g, offset=A_BYTES + g * K * 2)
             nc.sync.dma_start(out=a_raw[g][:], in_=a[bi, mt * P : (mt + 1) * P, :])
 
         def transpose_a(g):
             words = a_raw[g][:].bitcast(F32).rearrange("p (c w u) -> p c u w", c=PASSES, u=2)
-            a_grp[g] = agrp_pool.tile([P, PACK * K_PASS], BF16, name="a_grp", tag="a_grp", align_bytes=64)
-            grouped_w = a_grp[g][:].bitcast(F32).rearrange("p (c m u) -> p c m u", c=PASSES, u=2)
             for h in range(2):
-                xt = psum.tile([P, 2, 2, P], F32, name="xt", tag="bank")
+                xt[(g, h)] = psum.tile([P, 2, 2, P], F32, name="xt", tag="bank")
                 for ci in range(2):
                     for u in range(2):
-                        nc.tensor.transpose(xt[:, ci, u, :], words[:, 2 * h + ci, u, :], ident[:])
-                nc.scalar.copy(
-                    out=grouped_w[:, 2 * h : 2 * h + 2],
-                    in_=xt[:].rearrange("p c u m -> p c m u"),
-                )
+                        nc.tensor.transpose(xt[(g, h)][:, ci, u, :], words[:, 2 * h + ci, u, :], ident[:])
+
+        def mask_a(g):
+            a_grp[g] = agrp_pool.tile([P, PACK * K_PASS], BF16, name="a_grp", tag="a_grp", align_bytes=64)
+            grouped_w = a_grp[g][:].bitcast(F32).rearrange("p (c m u) -> p c m u", c=PASSES, u=2)
+            for c in range(PASSES):
+                h, ci = divmod(c, 2)
+                for j in range(2):
+                    rows = slice(64 * j, 64 * (j + 1))
+                    nc.scalar.activation(
+                        out=grouped_w[:, c, rows, :],
+                        in_=xt[(g, h)][:, ci, :, rows].rearrange("p u m -> p m u"),
+                        func=ACT.Copy,
+                        scale=keep[g // M_TILES][:, g % M_TILES, c, j : j + 1],
+                    )
 
         def magnitude(g):
             big[g] = awork.tile([P, K], BF16, name="big", tag="big")
@@ -101,43 +114,37 @@ def tile_sparsebmm_kernel(tc, a, b, out):
             )
 
         def count_columns(g):
-            cnt[g] = psum.tile([P, 16, 32], F32, name="cnt", tag="bank")
+            bi, mt = divmod(g, M_TILES)
+            if mt == 0:
+                cnt[bi] = psum.tile([P, M_TILES, 40], F32, name="cnt", tag="bank")
             for kc in range(16):
                 nc.tensor.matmul(
-                    out=cnt[g][:, kc, :],
+                    out=cnt[bi][:, mt, 2 * kc : 2 * kc + 2],
                     lhsT=big[g][:, kc * P : (kc + 1) * P],
                     rhs=sel[:],
                     start=True,
                     stop=True,
                 )
 
-        def count_tiles(g):
-            cnt_sb = awork.tile([P, 16, 2], BF16, name="cnt_sb", tag="cnt_sb", bufs=3)
-            nc.vector.tensor_copy(out=cnt_sb[:], in_=cnt[g][:, :, 0:2])
-            tot[g] = psum.tile([P, PASSES, 2], F32, name="tot", tag="bank")
-            cnt_by_q = cnt_sb[:].rearrange("p (c q) e -> p q c e", q=4)
+        def count_tiles(bi):
+            cnt_sb = awork.tile([P, M_TILES, 32], BF16, name="cnt_sb", tag="cnt_sb", bufs=2)
+            nc.vector.tensor_copy(out=cnt_sb[:], in_=cnt[bi][:, :, 0:32])
+            tot[bi] = cnt[bi][:, :, 32:40].rearrange("p m (c e) -> p m c e", e=2)
+            cnt_by_q = cnt_sb[:].rearrange("p m (c q e) -> p q m c e", q=4, e=2)
             for q in range(4):
                 nc.tensor.matmul(
-                    out=tot[g][:],
+                    out=tot[bi],
                     lhsT=spread[:, q, :],
                     rhs=cnt_by_q[:, q],
                     start=(q == 0),
                     stop=(q == 3),
                 )
 
-        def make_keep(g):
-            keep[g] = keep_pool.tile([P, PASSES, 2], F32, name="keep", tag="keep")
+        def make_keep(bi):
+            keep[bi] = keep_pool.tile([P, M_TILES, PASSES, 2], F32, name="keep", tag="keep")
             nc.vector.tensor_scalar(
-                out=keep[g][:], in0=tot[g][:], scalar1=0.5, scalar2=None, op0=ALU.is_gt
+                out=keep[bi][:], in0=tot[bi], scalar1=0.5, scalar2=None, op0=ALU.is_gt
             )
-
-        def mask_a(g):
-            for c in range(PASSES):
-                for j in range(2):
-                    part = a_grp[g][:, (2 * c + j) * 256 : (2 * c + j + 1) * 256]
-                    nc.vector.tensor_scalar(
-                        out=part, in0=part, scalar1=keep[g][:, c, j : j + 1], scalar2=None, op0=ALU.mult
-                    )
 
         def quantise_a(g):
             nc.vector.quantize_mx(
@@ -150,12 +157,12 @@ def tile_sparsebmm_kernel(tc, a, b, out):
             return ROUNDS[i // PASSES][2]
 
         def s_cols(i):
-            return S_COLS[i // PASSES] if i else width(i)
+            return S_COLS[i // PASSES] * min(i, 2) // 2
 
         def load_b(i):
             bi, n0, w = ROUNDS[i // PASSES]
             c = i % PASSES
-            raw = braw_pool.tile([P, PACK, w], BF16, name="b_raw%d" % i, offset=i * RAW_BYTES)
+            raw = raw_pool.tile([P, PACK, w], BF16, name="b_raw%d" % i, offset=i * RAW_BYTES)
             nc.sync.dma_start(
                 out=raw[:],
                 in_=b[bi, c * K_PASS : (c + 1) * K_PASS, n0 : n0 + w].rearrange("(p t) n -> p t n", t=PACK),
@@ -163,7 +170,8 @@ def tile_sparsebmm_kernel(tc, a, b, out):
             b_raw[i] = raw[:]
 
         def load_slab(c):
-            slab = braw_pool.tile([P, PACK, N], BF16, name="b_slab%d" % c, offset=2 * c * RAW_BYTES)
+            at = 2 * c * RAW_BYTES if c < 2 else A_BYTES + (c - 2) * 2 * RAW_BYTES
+            slab = raw_pool.tile([P, PACK, N], BF16, name="b_slab%d" % c, offset=at)
             nc.sync.dma_start(
                 out=slab[:],
                 in_=b[1, c * K_PASS : (c + 1) * K_PASS, :].rearrange("(p t) n -> p t n", t=PACK),
@@ -208,8 +216,8 @@ def tile_sparsebmm_kernel(tc, a, b, out):
                     in_=b_grp[i][:].rearrange("p n t -> p (n t)"),
                 )
                 b_q[i] = (codes, scales)
-                if i < N_B0 and i % 2 == 1:
-                    load_slab(i // 2)
+                if i in SLAB_BEHIND:
+                    load_slab(SLAB_BEHIND.index(i))
                 done["q"] = i + 1
 
         n_a = B * M_TILES
@@ -218,24 +226,29 @@ def tile_sparsebmm_kernel(tc, a, b, out):
                 load_a(g)
             for i in range(N_B0):
                 load_b(i)
-            for g in range(T_AHEAD):
-                transpose_a(g)
-            for s in range(n_a + 4):
-                if s < n_a:
-                    magnitude(s)
-                if 1 <= s <= n_a:
-                    flag_big(s - 1)
-                    count_columns(s - 1)
-                if 3 <= s <= n_a + 2:
-                    count_tiles(s - 3)
-                if 4 <= s:
-                    make_keep(s - 4)
-                if n_a <= s:
-                    mask_a(s - n_a)
-                if n_a + 2 <= s:
-                    quantise_a(s - n_a - 2)
-                if 1 <= s and s + T_AHEAD - 1 < n_a:
-                    transpose_a(s + T_AHEAD - 1)
+            magnitude(0)
+            flag_big(0)
+            count_columns(0)
+            magnitude(1)
+            for g in range(1, n_a):
+                if g + 1 < n_a:
+                    magnitude(g + 1)
+                flag_big(g)
+                if g == M_TILES:
+                    count_tiles(0)
+                    for mt in range(M_TILES):
+                        transpose_a(mt)
+                count_columns(g)
+                if g == M_TILES + 1:
+                    make_keep(0)
+                    for mt in range(M_TILES):
+                        mask_a(mt)
+            vector_up_to(1)
+            for mt in range(M_TILES):
+                quantise_a(mt)
+                if mt == 1:
+                    count_tiles(1)
+            make_keep(1)
             scalar_up_to(2)
 
         accs = {}
@@ -279,15 +292,14 @@ def tile_sparsebmm_kernel(tc, a, b, out):
             return 0 <= i < n_chunks and width(i) == 2 * N_TILE
 
         for i in range(n_chunks):
+            if i < 2:
+                for g in range(M_TILES + 2 * i, M_TILES + 2 * i + 2):
+                    transpose_a(g)
+                    mask_a(g)
             scalar_up_to(i + 1 + S_AHEAD)
-            if i == 0:
-                quantise_a(M_TILES - 2)
-                quantise_a(M_TILES - 1)
-            if i < M_TILES:
-                mask_a(M_TILES + i)
             vector_up_to(i + 1 + V_AHEAD)
-            if i < M_TILES:
-                quantise_a(M_TILES + i)
+            if 1 <= i <= M_TILES:
+                quantise_a(M_TILES + i - 1)
             quantise_up_to(i + 1 + Q_AHEAD)
             if wide(i - LAG):
                 multiply(i - LAG, (2, 3))

@@ -23,7 +23,7 @@ N_TILE = 512
 FLOPS = 2 * B * M * K * N
 
 ROUNDS = ((0, 0, 1024), (0, 1024, 1024), (1, 0, 1024), (1, 1024, 512), (1, 1536, 512))
-S_COLS = (704, 448, 416, 160, 96)
+S_COLS = (640, 416, 384, 160, 96)
 S_PIECE = 512
 N_B0 = 8
 RAW_BYTES = PACK * 1024 * 2

@@ -28,7 +28,7 @@ S_PIECE = 512
 N_B0 = 8
 RAW_BYTES = PACK * 1024 * 2
 A_BYTES = N_B0 * RAW_BYTES
-SLAB_BEHIND = (1, 3, 4, 5)
+SLAB_BEHIND = (1, 3, 3, 3)
 S_AHEAD = 3
 V_AHEAD = 2
 Q_AHEAD = 1
@@ -216,8 +216,9 @@ def tile_sparsebmm_kernel(tc, a, b, out):
                     in_=b_grp[i][:].rearrange("p n t -> p (n t)"),
                 )
                 b_q[i] = (codes, scales)
-                if i in SLAB_BEHIND:
-                    load_slab(SLAB_BEHIND.index(i))
+                for c in range(PASSES):
+                    if SLAB_BEHIND[c] == i:
+                        load_slab(c)
                 done["q"] = i + 1
 
         n_a = B * M_TILES

@@ -298,6 +298,8 @@ def tile_sparsebmm_kernel(tc, a, b, out):
                     transpose_a(g)
                     mask_a(g)
             scalar_up_to(i + 1 + S_AHEAD)
+            if i == n_chunks - 3:
+                quantise_up_to(i + 1 + Q_AHEAD)
             vector_up_to(i + 1 + V_AHEAD)
             if 1 <= i <= M_TILES:
                 quantise_a(M_TILES + i - 1)

from contextlib import ExitStack

import concourse.mybir as mybir
from concourse.masks import make_identity

F32 = mybir.dt.float32
BF16 = mybir.dt.bfloat16
I32 = mybir.dt.int32
U32 = mybir.dt.uint32
U8 = mybir.dt.uint8
FP8X4 = mybir.dt.float8_e4m3fn_x4
ALU = mybir.AluOpType
ACT = mybir.ActivationFunctionType

B, M, K, N = 2, 512, 2048, 2048
THRESHOLD = 1e-6
P = 128
PACK = 4
K_PASS = P * PACK
PASSES = K // K_PASS
M_TILES = M // P
N_TILE = 512
FLOPS = 2 * B * M * K * N

ROUNDS = ((0, 0, 1024), (0, 1024, 1024), (1, 0, 1024), (1, 1024, 512), (1, 1536, 512))
S_COLS = (640, 416, 384, 160, 96)
S_PIECE = 512
N_B0 = 8
RAW_BYTES = PACK * 1024 * 2
A_BYTES = N_B0 * RAW_BYTES
SLAB_BEHIND = (1, 3, 3, 3)
S_AHEAD = 3
V_AHEAD = 2
Q_AHEAD = 1
LAG = 2


def tile_sparsebmm_kernel(tc, a, b, out):
    nc = tc.nc
    n_chunks = len(ROUNDS) * PASSES
    with ExitStack() as ctx:
        const = ctx.enter_context(tc.tile_pool(name="const", bufs=1))
        awork = ctx.enter_context(tc.tile_pool(name="awork", bufs=4))
        agrp_pool = ctx.enter_context(tc.tile_pool(name="agrp", bufs=8))
        keep_pool = ctx.enter_context(tc.tile_pool(name="keep", bufs=2))
        raw_pool = ctx.enter_context(tc.tile_pool(name="raw", bufs=1))
        bgrp_pool = ctx.enter_context(tc.tile_pool(name="bgrp", bufs=5))
        bq_pool = ctx.enter_context(tc.tile_pool(name="bq", bufs=6))
        psum = ctx.enter_context(tc.psum_pool(name="psum", bufs=8))

        ident = const.tile([P, P], F32, name="ident")
        make_identity(nc, ident[:])
        halves = const.tile([P, 2], BF16, name="halves")
        nc.gpsimd.memset(halves[:], 0.0)
        nc.gpsimd.memset(halves[0:64, 0:1], 1.0)
        nc.gpsimd.memset(halves[64:128, 1:2], 1.0)
        one = const.tile([P, 1], F32, name="one")
        nc.gpsimd.memset(one[:], 1.0)
        sel = const.tile([P, 2], BF16, name="sel")
        nc.scalar.activation(out=sel[:].bitcast(F32), in_=halves[:].bitcast(F32), func=ACT.Copy, scale=one[:])
        spread = const.tile([P, 4, P], BF16, name="spread")
        nc.gpsimd.memset(spread[:], 0.0)
        for q in range(4):
            nc.gpsimd.memset(spread[0:64, q, 32 * q : 32 * q + 16], 1.0)
            nc.gpsimd.memset(spread[64:128, q, 32 * q + 16 : 32 * q + 32], 1.0)

        a_codes = const.tile([P, B * M_TILES, K_PASS], U32, name="a_codes", align_bytes=64)
        a_scales = const.tile([P, B * M_TILES, K_PASS], U8, name="a_scales", align_bytes=64)

        a_raw, big, xt, a_grp, cnt, tot, keep = {}, {}, {}, {}, {}, {}, {}
        b_raw, b_grp, b_q = {}, {}, {}
        done = {"rs": 0, "rv": 0, "q": 0}

        def load_a(g):
            bi, mt = divmod(g, M_TILES)
            a_raw[g] = raw_pool.tile([P, K], BF16, name="a_raw%d" % g, offset=A_BYTES + g * K * 2)
            nc.sync.dma_start(out=a_raw[g][:], in_=a[bi, mt * P : (mt + 1) * P, :])

        def transpose_a(g):
            words = a_raw[g][:].bitcast(F32).rearrange("p (c w u) -> p c u w", c=PASSES, u=2)
            for h in range(2):
                xt[(g, h)] = psum.tile([P, 2, 2, P], F32, name="xt", tag="bank")
                for ci in range(2):
                    for u in range(2):
                        nc.tensor.transpose(xt[(g, h)][:, ci, u, :], words[:, 2 * h + ci, u, :], ident[:])

        def mask_a(g):
            a_grp[g] = agrp_pool.tile([P, PACK * K_PASS], BF16, name="a_grp", tag="a_grp", align_bytes=64)
            grouped_w = a_grp[g][:].bitcast(F32).rearrange("p (c m u) -> p c m u", c=PASSES, u=2)
            for c in range(PASSES):
                h, ci = divmod(c, 2)
                for j in range(2):
                    rows = slice(64 * j, 64 * (j + 1))
                    nc.scalar.activation(
                        out=grouped_w[:, c, rows, :],
                        in_=xt[(g, h)][:, ci, :, rows].rearrange("p u m -> p m u"),
                        func=ACT.Copy,
                        scale=keep[g // M_TILES][:, g % M_TILES, c, j : j + 1],
                    )

        def magnitude(g):
            big[g] = awork.tile([P, K], BF16, name="big", tag="big")
            nc.vector.tensor_scalar(
                out=big[g][:].bitcast(I32),
                in0=a_raw[g][:].bitcast(I32),
                scalar1=0x7FFF7FFF,
                scalar2=None,
                op0=ALU.bitwise_and,
            )

        def flag_big(g):
            nc.vector.tensor_scalar(
                out=big[g][:], in0=big[g][:], scalar1=THRESHOLD, scalar2=None, op0=ALU.is_gt
            )

        def count_columns(g):
            bi, mt = divmod(g, M_TILES)
            if mt == 0:
                cnt[bi] = psum.tile([P, M_TILES, 40], F32, name="cnt", tag="bank")
            for kc in range(16):
                nc.tensor.matmul(
                    out=cnt[bi][:, mt, 2 * kc : 2 * kc + 2],
                    lhsT=big[g][:, kc * P : (kc + 1) * P],
                    rhs=sel[:],
                    start=True,
                    stop=True,
                )

        def count_tiles(bi):
            cnt_sb = awork.tile([P, M_TILES, 32], BF16, name="cnt_sb", tag="cnt_sb", bufs=2)
            nc.vector.tensor_copy(out=cnt_sb[:], in_=cnt[bi][:, :, 0:32])
            tot[bi] = cnt[bi][:, :, 32:40].rearrange("p m (c e) -> p m c e", e=2)
            cnt_by_q = cnt_sb[:].rearrange("p m (c q e) -> p q m c e", q=4, e=2)
            for q in range(4):
                nc.tensor.matmul(
                    out=tot[bi],
                    lhsT=spread[:, q, :],
                    rhs=cnt_by_q[:, q],
                    start=(q == 0),
                    stop=(q == 3),
                )

        def make_keep(bi):
            keep[bi] = keep_pool.tile([P, M_TILES, PASSES, 2], F32, name="keep", tag="keep")
            nc.vector.tensor_scalar(
                out=keep[bi][:], in0=tot[bi], scalar1=0.5, scalar2=None, op0=ALU.is_gt
            )

        def quantise_a(g):
            nc.vector.quantize_mx(
                out=a_codes[:, g, :].bitcast(FP8X4),
                scales=a_scales[:, g, :],
                in_=a_grp[g][:],
            )

        def width(i):
            return ROUNDS[i // PASSES][2]

        def s_cols(i):
            return S_COLS[i // PASSES] * min(i, 2) // 2

        def load_b(i):
            bi, n0, w = ROUNDS[i // PASSES]
            c = i % PASSES
            raw = raw_pool.tile([P, PACK, w], BF16, name="b_raw%d" % i, offset=i * RAW_BYTES)
            nc.sync.dma_start(
                out=raw[:],
                in_=b[bi, c * K_PASS : (c + 1) * K_PASS, n0 : n0 + w].rearrange("(p t) n -> p t n", t=PACK),
            )
            b_raw[i] = raw[:]

        def load_slab(c):
            at = 2 * c * RAW_BYTES if c < 2 else A_BYTES + (c - 2) * 2 * RAW_BYTES
            slab = raw_pool.tile([P, PACK, N], BF16, name="b_slab%d" % c, offset=at)
            nc.sync.dma_start(
                out=slab[:],
                in_=b[1, c * K_PASS : (c + 1) * K_PASS, :].rearrange("(p t) n -> p t n", t=PACK),
            )
            for r in range(N_B0 // PASSES, len(ROUNDS)):
                n0, w = ROUNDS[r][1], ROUNDS[r][2]
                b_raw[r * PASSES + c] = slab[:, :, n0 : n0 + w]

        def grouped_b(i):
            if i not in b_grp:
                b_grp[i] = bgrp_pool.tile([P, width(i), PACK], BF16, name="b_grp", tag="b_grp", align_bytes=64)
            return b_grp[i]

        def regroup(engine_copy, i, lo, hi):
            engine_copy(
                out=grouped_b(i)[:, lo:hi, :].rearrange("p (c i) t -> p c t i", i=4),
                in_=b_raw[i][:, :, lo:hi].rearrange("p t (c i) -> p c t i", i=4),
            )

        def scalar_up_to(n):
            for i in range(done["rs"], min(n, n_chunks)):
                for lo in range(width(i) - s_cols(i), width(i), S_PIECE):
                    regroup(nc.scalar.copy, i, lo, min(lo + S_PIECE, width(i)))
                done["rs"] = i + 1

        def vector_up_to(n):
            for i in range(done["rv"], min(n, n_chunks)):
                if s_cols(i) < width(i):
                    regroup(nc.vector.tensor_copy, i, 0, width(i) - s_cols(i))
                done["rv"] = i + 1

        def quantise_up_to(n):
            for i in range(done["q"], min(n, n_chunks)):
                scalar_up_to(i + 1)
                vector_up_to(i + 1)
                w = width(i)
                codes = bq_pool.tile([P, w], U32, name="b_codes", tag="b_codes", align_bytes=64)
                scales = bq_pool.tile([P, w], U8, name="b_scales", tag="b_scales", align_bytes=64)
                nc.vector.quantize_mx(
                    out=codes[:].bitcast(FP8X4),
                    scales=scales[:],
                    in_=b_grp[i][:].rearrange("p n t -> p (n t)"),
                )
                b_q[i] = (codes, scales)
                for c in range(PASSES):
                    if SLAB_BEHIND[c] == i:
                        load_slab(c)
                done["q"] = i + 1

        n_a = B * M_TILES
        with tc.manual_schedule():
            for g in range(n_a):
                load_a(g)
            for i in range(N_B0):
                load_b(i)
            magnitude(0)
            flag_big(0)
            count_columns(0)
            magnitude(1)
            for g in range(1, n_a):
                if g + 1 < n_a:
                    magnitude(g + 1)
                flag_big(g)
                if g == M_TILES:
                    count_tiles(0)
                    for mt in range(M_TILES):
                        transpose_a(mt)
                count_columns(g)
                if g == M_TILES + 1:
                    make_keep(0)
                    for mt in range(M_TILES):
                        mask_a(mt)
            vector_up_to(1)
            for mt in range(M_TILES):
                quantise_a(mt)
                if mt == 1:
                    count_tiles(1)
            make_keep(1)
            scalar_up_to(2)

        accs = {}

        def multiply(i, m_tiles):
            r, c = divmod(i, PASSES)
            bi, n0, w = ROUNDS[r]
            n_tiles = w // N_TILE
            if c == 0:
                for mt in m_tiles:
                    for nt in range(n_tiles):
                        acc = psum.tile([P, N_TILE], F32, name="acc", tag="bank")
                        accs[(r, mt, nt)] = acc
            codes, scales = b_q[i]
            for mt in m_tiles:
                g = bi * M_TILES + mt
                for nt in range(n_tiles):
                    nc.tensor.matmul_mx(
                        out=accs[(r, mt, nt)][:],
                        lhsT=a_codes[:, g, c * P : (c + 1) * P].bitcast(FP8X4),
                        lhsT_scale=a_scales[:, g, c * P : (c + 1) * P],
                        rhs=codes[:, nt * N_TILE : (nt + 1) * N_TILE].bitcast(FP8X4),
                        rhs_scale=scales[:, nt * N_TILE : (nt + 1) * N_TILE],
                        start=(c == 0),
                        stop=(c == PASSES - 1),
                    )
            if c == PASSES - 1:
                for mt in m_tiles:
                    on_vector = r == len(ROUNDS) - 1 and mt % 2 == 1
                    stage = agrp_pool.tile([P, w], F32, name="stage", tag="a_grp", align_bytes=64)
                    for nt in range(n_tiles):
                        dst = stage[:, nt * N_TILE : (nt + 1) * N_TILE]
                        if on_vector:
                            nc.vector.tensor_copy(out=dst, in_=accs[(r, mt, nt)][:])
                        else:
                            nc.scalar.copy(out=dst, in_=accs[(r, mt, nt)][:])
                    rows = out[bi, mt * P : (mt + 1) * P, n0 : n0 + w]
                    nc.sync.dma_start(out=rows, in_=stage[:])

        def wide(i):
            return 0 <= i < n_chunks and width(i) == 2 * N_TILE

        for i in range(n_chunks):
            if i < 2:
                for g in range(M_TILES + 2 * i, M_TILES + 2 * i + 2):
                    transpose_a(g)
                    mask_a(g)
            scalar_up_to(i + 1 + S_AHEAD)
            if i == n_chunks - 3:
                quantise_up_to(i + 1 + Q_AHEAD)
            vector_up_to(i + 1 + V_AHEAD)
            if 1 <= i <= M_TILES:
                quantise_a(M_TILES + i - 1)
            quantise_up_to(i + 1 + Q_AHEAD)
            if wide(i - LAG):
                multiply(i - LAG, (2, 3))
            if wide(i):
                multiply(i, (0, 1))
            else:
                multiply(i, (0, 1, 2, 3))
